import numpy as np
import ml_dtypes


def mxq(x, axis, fmt="e4m3"):
    dtype, down = {"e4m3": (ml_dtypes.float8_e4m3fn, 7), "e5m2": (ml_dtypes.float8_e5m2, 14)}[fmt]
    v = np.moveaxis(np.asarray(x, np.float32).astype(ml_dtypes.bfloat16).astype(np.float64), axis, -1)
    blocks = v.reshape(v.shape[:-1] + (-1, 32))
    amax = np.abs(blocks).max(-1, keepdims=True)
    byte = np.maximum(np.where(amax > 0, np.frexp(amax)[1] - 1 + 127, 0) - down, 1)
    scale = np.exp2(byte - 127.0)
    codes = (blocks / scale).astype(np.float32).astype(dtype).astype(np.float64)
    return np.moveaxis((codes * scale).reshape(v.shape), -1, axis)


WIDE = False


def mx_kscale(k):
    if not WIDE:
        return np.ones(k)
    levels = np.array([10, -10, 5, -5, 0])
    a = np.random.permutation(np.resize(levels, k // 512 * 4)).reshape(k // 512, 4)
    idx = np.arange(k)
    return np.exp2(a[idx // 512, idx % 128 // 32])


BF16 = ml_dtypes.bfloat16


def bf(x):
    return np.asarray(x, np.float32).astype(BF16)


def f64(x):
    return np.asarray(x).astype(np.float64)


B, S, D, DV, NS, SD = 4, 128, 1024, 1024, 4, 256
R = B * S


def silu(v):
    return v / (1.0 + np.exp(-v))


def setup_inputs():
    s, r, t = mx_kscale(D), mx_kscale(D), mx_kscale(DV)
    return {"x": bf(np.random.standard_normal((B, S, D)) * r),
            "h": bf(np.random.standard_normal((B, S, D)) * s),
            "Wv": bf(np.random.standard_normal((NS, DV, D)) / np.sqrt(D) * t[:, None] / s),
            "W1": bf(np.random.standard_normal((NS, SD, D + DV)) / np.sqrt(D + DV) / np.concatenate([r, t]))}


def reference(x, h, Wv, W1):
    xf = f64(x).reshape(R, D)
    hf = f64(h).reshape(R, D)
    w1 = f64(W1)
    views = mxq(hf, 1, "e4m3") @ mxq(f64(Wv).transpose(0, 2, 1), 1, "e4m3")
    a = mxq(xf, 1, "e4m3") @ mxq(w1[:, :, :D].transpose(0, 2, 1), 1, "e4m3")
    b = mxq(views, 2, "e4m3") @ mxq(w1[:, :, D:].transpose(0, 2, 1), 1, "e4m3")
    return silu(a + b).reshape(NS, B, S, SD)

@@ -1,0 +1,235 @@
+from contextlib import ExitStack
+
+import concourse.mybir as mybir
+from concourse.masks import make_identity
+
+F32 = mybir.dt.float32
+BF16 = mybir.dt.bfloat16
+U32 = mybir.dt.uint32
+U8 = mybir.dt.uint8
+FP8X4 = mybir.dt.float8_e4m3fn_x4
+SILU = mybir.ActivationFunctionType.Silu
+
+P = 128
+NS = 4
+R = 512
+D = 1024
+DV = 1024
+SD = 256
+FLOPS = 2 * NS * R * (D * DV + (D + DV) * SD)
+
+
+def tile_distributedb_pa_kernel(tc, x, h, Wv, W1, out):
+    nc = tc.nc
+    with ExitStack() as ctx:
+        const = ctx.enter_context(tc.tile_pool(name="const", bufs=1))
+        inputs = ctx.enter_context(tc.tile_pool(name="inputs", bufs=1))
+        stage = ctx.enter_context(tc.tile_pool(name="stage", bufs=3))
+        keep = ctx.enter_context(tc.tile_pool(name="keep", bufs=1))
+        pair = ctx.enter_context(tc.tile_pool(name="pair", bufs=2))
+        psum = ctx.enter_context(tc.psum_pool(name="psum", bufs=8))
+        ctx.enter_context(tc.manual_schedule())
+
+        h_sb = inputs.tile([P, 4 * D], BF16, name="h_sb")
+        x_sb = inputs.tile([P, 4 * D], BF16, name="x_sb")
+        wv_sb = [inputs.tile([P, 8 * D], BF16, name="wv_sb%d" % s) for s in range(NS)]
+        w1_sb = [inputs.tile([P, 2 * (D + DV)], BF16, name="w1_sb%d" % s) for s in range(NS)]
+
+        def load_rows(dst, src):
+            view = src.flatten_outer_dims().rearrange("(m j) d -> m (j d)", j=4)
+            for half in range(2):
+                cols = slice(2 * D * half, 2 * D * (half + 1))
+                nc.sync.dma_start(out=dst[:, cols], in_=view[:, cols])
+
+        def load_wv(s, gp):
+            for u in range(2):
+                first = 512 * gp + 256 * u
+                tile0 = 4 * gp + 2 * u
+                nc.sync.dma_start(
+                    out=wv_sb[s][:, tile0 * D : (tile0 + 2) * D],
+                    in_=Wv[s, first : first + 256, :].rearrange("(m e) d -> m (e d)", e=2),
+                )
+
+        def load_w1(s):
+            nc.sync.dma_start(
+                out=w1_sb[s][:].rearrange("m (a k) -> m a k", a=2),
+                in_=W1[s].rearrange("(a m) k -> m a k", a=2),
+            )
+
+        load_rows(h_sb, h)
+        load_wv(0, 0)
+        load_wv(0, 1)
+        load_wv(1, 0)
+        load_w1(0)
+        load_rows(x_sb, x)
+        load_wv(1, 1)
+        load_wv(2, 0)
+        load_w1(1)
+        load_wv(2, 1)
+        load_wv(3, 0)
+        load_w1(2)
+        load_wv(3, 1)
+        load_w1(3)
+
+        ident = const.tile([P, P], F32, name="ident")
+        make_identity(nc, ident[:])
+        zero = const.tile([P, 1], F32, name="zero")
+        nc.vector.memset(zero[:], 0.0)
+        warm = const.tile([P, 1], F32, name="warm")
+        nc.scalar.activation(out=warm[:], in_=zero[:], func=SILU)
+
+        def copy_out(engine, dst, src):
+            if engine == "V":
+                nc.vector.tensor_copy(out=dst, in_=src)
+            else:
+                nc.scalar.copy(out=dst, in_=src)
+
+        def flush(late):
+            if late is not None:
+                late()
+
+        def transpose_round(src, tile_words, banks, codes, scales, engines, late):
+            words = src[:].bitcast(F32)
+            grouped = stage.tile([P, 4096], BF16, tag="grouped", align_bytes=64)
+            grouped_words = grouped[:].bitcast(F32)
+            for n, (slot, first_tile, k_pass) in enumerate(banks):
+                bank = psum.tile([P, 512], F32, tag="bank")
+                for u in range(2):
+                    for i in range(2):
+                        w0 = (first_tile + i) * tile_words + 256 * k_pass + 128 * u
+                        c0 = 256 * u + 128 * i
+                        nc.tensor.transpose(bank[:, c0 : c0 + 128], words[:, w0 : w0 + 128], ident[:])
+                copy_out(
+                    engines[n],
+                    grouped_words[:, 512 * slot : 512 * (slot + 1)].rearrange("p (c u) -> p c u", u=2),
+                    bank[:].rearrange("p (u c) -> p c u", u=2),
+                )
+                if n == 0:
+                    flush(late)
+            return lambda: nc.vector.quantize_mx(
+                out=codes[:].bitcast(FP8X4), scales=scales[:], in_=grouped[:]
+            )
+
+        def four_tiles(tile0):
+            return [(0, tile0, 0), (2, tile0, 1), (1, tile0 + 2, 0), (3, tile0 + 2, 1)]
+
+        h_codes = keep.tile([P, 1024], U32, name="h_codes", align_bytes=64)
+        h_scales = keep.tile([P, 1024], U8, name="h_scales", align_bytes=64)
+        x_codes = keep.tile([P, 1024], U32, name="x_codes", align_bytes=64)
+        x_scales = keep.tile([P, 1024], U8, name="x_scales", align_bytes=64)
+        wv_q = {}
+        w1_q = {}
+        views_q = {}
+
+        def wv_round(s, gp, engines, late):
+            wv_codes = pair.tile([P, 1024], U32, tag="wv_codes%d" % gp, align_bytes=64)
+            wv_scales = pair.tile([P, 1024], U8, tag="wv_scales%d" % gp, align_bytes=64)
+            wv_q[(s, gp)] = (wv_codes, wv_scales)
+            return transpose_round(wv_sb[s], 512, four_tiles(4 * gp), wv_codes, wv_scales, engines, late)
+
+        def w1_round(s, engines, late):
+            w1_codes = pair.tile([P, 1024], U32, tag="w1_codes", align_bytes=64)
+            w1_scales = pair.tile([P, 1024], U8, tag="w1_scales", align_bytes=64)
+            w1_q[s] = (w1_codes, w1_scales)
+            banks = [(n, 0, n) for n in range(4)]
+            return transpose_round(w1_sb[s], 1024, banks, w1_codes, w1_scales, engines, late)
+
+        def views_round(s, gp, engines, late, fine):
+            wv_codes, wv_scales = wv_q[(s, gp)]
+            v_grouped = pair.tile([P, 2048], BF16, tag="v_grouped%d" % gp, align_bytes=64)
+            v_codes = pair.tile([P, 512], U32, tag="v_codes%d" % gp, align_bytes=64)
+            v_scales = pair.tile([P, 512], U8, tag="v_scales%d" % gp, align_bytes=64)
+            views_q[(s, gp)] = (v_codes, v_scales)
+
+            def quantise(j0, j1):
+                nc.vector.quantize_mx(
+                    out=v_codes[:, 128 * j0 : 128 * j1].bitcast(FP8X4),
+                    scales=v_scales[:, 128 * j0 : 128 * j1],
+                    in_=v_grouped[:, 512 * j0 : 512 * j1],
+                )
+
+            for j in range(4):
+                bank = psum.tile([P, 512], F32, tag="bank")
+                for t in range(4):
+                    for g in range(2):
+                        wc = slice(512 * g + 128 * t, 512 * g + 128 * (t + 1))
+                        hc = slice(512 * g + 128 * j, 512 * g + 128 * (j + 1))
+                        nc.tensor.matmul_mx(
+                            out=bank[:, 128 * t : 128 * (t + 1)],
+                            lhsT=wv_codes[:, wc].bitcast(FP8X4),
+                            lhsT_scale=wv_scales[:, wc],
+                            rhs=h_codes[:, hc].bitcast(FP8X4),
+                            rhs_scale=h_scales[:, hc],
+                            start=(g == 0),
+                            stop=(g == 1),
+                        )
+                copy_out(
+                    engines[j],
+                    v_grouped[:, 512 * j : 512 * (j + 1)].rearrange("p (c t) -> p c t", t=4),
+                    bank[:].rearrange("p (t c) -> p c t", t=4),
+                )
+                if j == 0:
+                    flush(late)
+                if fine and j > 0:
+                    quantise(j - 1, j)
+            if fine:
+                quantise(3, 4)
+                return None
+            return lambda: quantise(0, 4)
+
+        def out_round(s, late, fine):
+            w1_codes, w1_scales = w1_q[s]
+            o_sb = pair.tile([P, 4 * SD], F32, tag="o_sb")
+            o_view = out[s].rearrange("b q f -> (b q) f").rearrange("(m j) f -> m (j f)", j=4)
+            bank = None
+            for j in range(4):
+                if fine or j % 2 == 0:
+                    bank = psum.tile([P, 512], F32, tag="bank")
+                c0 = 0 if fine else 256 * (j % 2)
+                operands = [(x_codes, x_scales, 512 * g + 128 * j) for g in range(2)]
+                operands.extend([views_q[(s, gp)] + (128 * j,) for gp in range(2)])
+                for n, (codes, scales, col) in enumerate(operands):
+                    nc.tensor.matmul_mx(
+                        out=bank[:, c0 : c0 + 256],
+                        lhsT=codes[:, col : col + 128].bitcast(FP8X4),
+                        lhsT_scale=scales[:, col : col + 128],
+                        rhs=w1_codes[:, 256 * n : 256 * (n + 1)].bitcast(FP8X4),
+                        rhs_scale=w1_scales[:, 256 * n : 256 * (n + 1)],
+                        start=(n == 0),
+                        stop=(n == 3),
+                    )
+                if fine:
+                    cols = slice(256 * j, 256 * (j + 1))
+                    nc.scalar.activation(out=o_sb[:, cols], in_=bank[:, 0:256], func=SILU)
+                    nc.sync.dma_start(out=o_view[:, cols], in_=o_sb[:, cols])
+                elif j % 2 == 1:
+                    cols = slice(256 * (j - 1), 256 * (j + 1))
+                    nc.scalar.activation(out=o_sb[:, cols], in_=bank[:], func=SILU)
+                if j == 1:
+                    flush(late)
+            if not fine:
+                nc.sync.dma_start(out=o_view, in_=o_sb[:])
+            return None
+
+        T_ENG = "VSSS"
+        V_ENG = "VSVS"
+        flush(transpose_round(h_sb, 512, four_tiles(0), h_codes, h_scales, "VSVS", None))
+        flush(wv_round(0, 0, "VSVS", None))
+        late = wv_round(0, 1, "VSVS", None)
+        late = views_round(0, 0, V_ENG, late, False)
+        late = wv_round(1, 0, T_ENG, late)
+        late = views_round(0, 1, V_ENG, late, False)
+        late = w1_round(0, T_ENG, late)
+        late = transpose_round(x_sb, 512, four_tiles(0), x_codes, x_scales, T_ENG, late)
+        for s in range(1, NS):
+            late = views_round(s, 0, V_ENG, late, False)
+            late = wv_round(s, 1, T_ENG, late)
+            late = out_round(s - 1, late, False)
+            if s + 1 < NS:
+                late = wv_round(s + 1, 0, T_ENG, late)
+                late = views_round(s, 1, V_ENG, late, False)
+                late = w1_round(s, T_ENG, late)
+            else:
+                flush(w1_round(s, T_ENG, late))
+                views_round(s, 1, "SSSV", None, True)
+        out_round(NS - 1, None, True)

@@ -59,17 +59,12 @@ def tile_distributedb_pa_kernel(tc, x, h, Wv, W1, out):
         load_rows(h_sb, h)
         load_wv(0, 0)
         load_wv(0, 1)
-        load_wv(1, 0)
         load_w1(0)
         load_rows(x_sb, x)
-        load_wv(1, 1)
-        load_wv(2, 0)
-        load_w1(1)
-        load_wv(2, 1)
-        load_wv(3, 0)
-        load_w1(2)
-        load_wv(3, 1)
-        load_w1(3)
+        for s in range(1, NS):
+            load_wv(s, 0)
+            load_wv(s, 1)
+            load_w1(s)
 
         ident = const.tile([P, P], F32, name="ident")
         make_identity(nc, ident[:])
@@ -217,19 +212,20 @@ def tile_distributedb_pa_kernel(tc, x, h, Wv, W1, out):
         flush(wv_round(0, 0, "VSVS", None))
         late = wv_round(0, 1, "VSVS", None)
         late = views_round(0, 0, V_ENG, late, False)
-        late = wv_round(1, 0, T_ENG, late)
         late = views_round(0, 1, V_ENG, late, False)
         late = w1_round(0, T_ENG, late)
         late = transpose_round(x_sb, 512, four_tiles(0), x_codes, x_scales, T_ENG, late)
         for s in range(1, NS):
-            late = views_round(s, 0, V_ENG, late, False)
+            if s > 1:
+                late = w1_round(s - 1, T_ENG, late)
+            late = wv_round(s, 0, T_ENG, late)
             late = wv_round(s, 1, T_ENG, late)
-            late = out_round(s - 1, late, False)
-            if s + 1 < NS:
-                late = wv_round(s + 1, 0, T_ENG, late)
-                late = views_round(s, 1, V_ENG, late, False)
+            if s == NS - 1:
                 late = w1_round(s, T_ENG, late)
+            late = out_round(s - 1, late, False)
+            late = views_round(s, 0, V_ENG, late, False)
+            if s < NS - 1:
+                late = views_round(s, 1, V_ENG, late, False)
             else:
-                flush(w1_round(s, T_ENG, late))
-                views_round(s, 1, "SSSV", None, True)
+                views_round(s, 1, "SSSV", late, True)
         out_round(NS - 1, None, True)

@@ -59,12 +59,17 @@ def tile_distributedb_pa_kernel(tc, x, h, Wv, W1, out):
         load_rows(h_sb, h)
         load_wv(0, 0)
         load_wv(0, 1)
+        load_wv(1, 0)
         load_w1(0)
         load_rows(x_sb, x)
-        for s in range(1, NS):
-            load_wv(s, 0)
-            load_wv(s, 1)
-            load_w1(s)
+        load_wv(1, 1)
+        load_wv(2, 0)
+        load_w1(1)
+        load_wv(2, 1)
+        load_wv(3, 0)
+        load_w1(2)
+        load_wv(3, 1)
+        load_w1(3)
 
         ident = const.tile([P, P], F32, name="ident")
         make_identity(nc, ident[:])
@@ -143,14 +148,16 @@ def tile_distributedb_pa_kernel(tc, x, h, Wv, W1, out):
                     in_=v_grouped[:, 512 * j0 : 512 * j1],
                 )
 
-            for j in range(4):
+            for n in range(4):
+                half, tp = n // 2, n % 2
                 bank = psum.tile([P, 512], F32, tag="bank")
-                for t in range(4):
+                for i in range(2):
+                    t = 2 * tp + i
                     for g in range(2):
                         wc = slice(512 * g + 128 * t, 512 * g + 128 * (t + 1))
-                        hc = slice(512 * g + 128 * j, 512 * g + 128 * (j + 1))
+                        hc = slice(512 * g + 256 * half, 512 * g + 256 * (half + 1))
                         nc.tensor.matmul_mx(
-                            out=bank[:, 128 * t : 128 * (t + 1)],
+                            out=bank[:, 256 * i : 256 * (i + 1)],
                             lhsT=wv_codes[:, wc].bitcast(FP8X4),
                             lhsT_scale=wv_scales[:, wc],
                             rhs=h_codes[:, hc].bitcast(FP8X4),
@@ -159,16 +166,18 @@ def tile_distributedb_pa_kernel(tc, x, h, Wv, W1, out):
                             stop=(g == 1),
                         )
                 copy_out(
-                    engines[j],
-                    v_grouped[:, 512 * j : 512 * (j + 1)].rearrange("p (c t) -> p c t", t=4),
-                    bank[:].rearrange("p (t c) -> p c t", t=4),
+                    engines[n],
+                    v_grouped[:, 1024 * half : 1024 * (half + 1)].rearrange("p (c t) -> p c t", t=4)[
+                        :, :, 2 * tp : 2 * tp + 2
+                    ],
+                    bank[:].rearrange("p (t c) -> p c t", t=2),
                 )
-                if j == 0:
+                if n == 0:
                     flush(late)
-                if fine and j > 0:
-                    quantise(j - 1, j)
+                if fine and n == 2:
+                    quantise(0, 2)
             if fine:
-                quantise(3, 4)
+                quantise(2, 4)
                 return None
             return lambda: quantise(0, 4)
 
@@ -207,25 +216,24 @@ def tile_distributedb_pa_kernel(tc, x, h, Wv, W1, out):
             return None
 
         T_ENG = "VSSS"
-        V_ENG = "VSVS"
+        V_ENG = "VVSS"
         flush(transpose_round(h_sb, 512, four_tiles(0), h_codes, h_scales, "VSVS", None))
         flush(wv_round(0, 0, "VSVS", None))
         late = wv_round(0, 1, "VSVS", None)
         late = views_round(0, 0, V_ENG, late, False)
+        late = wv_round(1, 0, T_ENG, late)
         late = views_round(0, 1, V_ENG, late, False)
         late = w1_round(0, T_ENG, late)
         late = transpose_round(x_sb, 512, four_tiles(0), x_codes, x_scales, T_ENG, late)
         for s in range(1, NS):
-            if s > 1:
-                late = w1_round(s - 1, T_ENG, late)
-            late = wv_round(s, 0, T_ENG, late)
-            late = wv_round(s, 1, T_ENG, late)
-            if s == NS - 1:
-                late = w1_round(s, T_ENG, late)
-            late = out_round(s - 1, late, False)
             late = views_round(s, 0, V_ENG, late, False)
-            if s < NS - 1:
+            late = wv_round(s, 1, T_ENG, late)
+            late = out_round(s - 1, late, False)
+            if s + 1 < NS:
+                late = wv_round(s + 1, 0, T_ENG, late)
                 late = views_round(s, 1, V_ENG, late, False)
+                late = w1_round(s, T_ENG, late)
             else:
-                views_round(s, 1, "SSSV", late, True)
+                flush(w1_round(s, T_ENG, late))
+                views_round(s, 1, "SSVV", None, True)
         out_round(NS - 1, None, True)

@@ -35,11 +35,10 @@ def tile_distributedb_pa_kernel(tc, x, h, Wv, W1, out):
         wv_sb = [inputs.tile([P, 8 * D], BF16, name="wv_sb%d" % s) for s in range(NS)]
         w1_sb = [inputs.tile([P, 2 * (D + DV)], BF16, name="w1_sb%d" % s) for s in range(NS)]
 
-        def load_rows(dst, src):
+        def load_rows(dst, src, half):
             view = src.flatten_outer_dims().rearrange("(m j) d -> m (j d)", j=4)
-            for half in range(2):
-                cols = slice(2 * D * half, 2 * D * (half + 1))
-                nc.sync.dma_start(out=dst[:, cols], in_=view[:, cols])
+            cols = slice(2 * D * half, 2 * D * (half + 1))
+            nc.sync.dma_start(out=dst[:, cols], in_=view[:, cols])
 
         def load_wv(s, gp):
             for u in range(2):
@@ -51,25 +50,24 @@ def tile_distributedb_pa_kernel(tc, x, h, Wv, W1, out):
                 )
 
         def load_w1(s):
-            nc.sync.dma_start(
-                out=w1_sb[s][:].rearrange("m (a k) -> m a k", a=2),
-                in_=W1[s].rearrange("(a m) k -> m a k", a=2),
-            )
+            for half in range(2):
+                cols = slice(D * half, D * (half + 1))
+                nc.sync.dma_start(
+                    out=w1_sb[s][:].rearrange("m (a k) -> m a k", a=2)[:, :, cols],
+                    in_=W1[s].rearrange("(a m) k -> m a k", a=2)[:, :, cols],
+                )
 
-        load_rows(h_sb, h)
+        load_rows(h_sb, h, 0)
         load_wv(0, 0)
+        load_rows(h_sb, h, 1)
         load_wv(0, 1)
-        load_wv(1, 0)
+        load_rows(x_sb, x, 0)
+        load_rows(x_sb, x, 1)
         load_w1(0)
-        load_rows(x_sb, x)
-        load_wv(1, 1)
-        load_wv(2, 0)
-        load_w1(1)
-        load_wv(2, 1)
-        load_wv(3, 0)
-        load_w1(2)
-        load_wv(3, 1)
-        load_w1(3)
+        for s in range(1, NS):
+            load_wv(s, 0)
+            load_wv(s, 1)
+            load_w1(s)
 
         ident = const.tile([P, P], F32, name="ident")
         make_identity(nc, ident[:])
@@ -88,11 +86,12 @@ def tile_distributedb_pa_kernel(tc, x, h, Wv, W1, out):
             if late is not None:
                 late()
 
-        def transpose_round(src, tile_words, banks, codes, scales, engines, late):
+        def transpose_round(src, tile_words, banks, codes, scales, col0, engines, late):
             words = src[:].bitcast(F32)
-            grouped = stage.tile([P, 4096], BF16, tag="grouped", align_bytes=64)
+            n_banks = len(banks)
+            grouped = stage.tile([P, 1024 * n_banks], BF16, tag="grouped", align_bytes=64)
             grouped_words = grouped[:].bitcast(F32)
-            for n, (slot, first_tile, k_pass) in enumerate(banks):
+            for n, (first_tile, k_pass) in enumerate(banks):
                 bank = psum.tile([P, 512], F32, tag="bank")
                 for u in range(2):
                     for i in range(2):
@@ -101,17 +100,21 @@ def tile_distributedb_pa_kernel(tc, x, h, Wv, W1, out):
                         nc.tensor.transpose(bank[:, c0 : c0 + 128], words[:, w0 : w0 + 128], ident[:])
                 copy_out(
                     engines[n],
-                    grouped_words[:, 512 * slot : 512 * (slot + 1)].rearrange("p (c u) -> p c u", u=2),
+                    grouped_words[:, 512 * n : 512 * (n + 1)].rearrange("p (c u) -> p c u", u=2),
                     bank[:].rearrange("p (u c) -> p c u", u=2),
                 )
                 if n == 0:
                     flush(late)
+            cols = slice(col0, col0 + 256 * n_banks)
             return lambda: nc.vector.quantize_mx(
-                out=codes[:].bitcast(FP8X4), scales=scales[:], in_=grouped[:]
+                out=codes[:, cols].bitcast(FP8X4), scales=scales[:, cols], in_=grouped[:]
             )
 
-        def four_tiles(tile0):
-            return [(0, tile0, 0), (2, tile0, 1), (1, tile0 + 2, 0), (3, tile0 + 2, 1)]
+        def tile_pairs(tile0, pairs):
+            return [(tile0 + 2 * q, g) for q in pairs for g in range(2)]
+
+        def column(tile, g):
+            return 512 * (tile // 2) + 256 * g + 128 * (tile % 2)
 
         h_codes = keep.tile([P, 1024], U32, name="h_codes", align_bytes=64)
         h_scales = keep.tile([P, 1024], U8, name="h_scales", align_bytes=64)
@@ -121,43 +124,50 @@ def tile_distributedb_pa_kernel(tc, x, h, Wv, W1, out):
         w1_q = {}
         views_q = {}
 
-        def wv_round(s, gp, engines, late):
-            wv_codes = pair.tile([P, 1024], U32, tag="wv_codes%d" % gp, align_bytes=64)
-            wv_scales = pair.tile([P, 1024], U8, tag="wv_scales%d" % gp, align_bytes=64)
-            wv_q[(s, gp)] = (wv_codes, wv_scales)
-            return transpose_round(wv_sb[s], 512, four_tiles(4 * gp), wv_codes, wv_scales, engines, late)
+        def rows_round(src, codes, scales, pairs, engines, late):
+            return transpose_round(src, 512, tile_pairs(0, pairs), codes, scales, 512 * pairs[0], engines, late)
+
+        def wv_round(s, gp, pairs, engines, late):
+            if (s, gp) not in wv_q:
+                wv_codes = pair.tile([P, 1024], U32, tag="wv_codes%d" % gp, align_bytes=64)
+                wv_scales = pair.tile([P, 1024], U8, tag="wv_scales%d" % gp, align_bytes=64)
+                wv_q[(s, gp)] = (wv_codes, wv_scales)
+            codes, scales = wv_q[(s, gp)]
+            return transpose_round(
+                wv_sb[s], 512, tile_pairs(4 * gp, pairs), codes, scales, 512 * pairs[0], engines, late
+            )
 
         def w1_round(s, engines, late):
             w1_codes = pair.tile([P, 1024], U32, tag="w1_codes", align_bytes=64)
             w1_scales = pair.tile([P, 1024], U8, tag="w1_scales", align_bytes=64)
             w1_q[s] = (w1_codes, w1_scales)
-            banks = [(n, 0, n) for n in range(4)]
-            return transpose_round(w1_sb[s], 1024, banks, w1_codes, w1_scales, engines, late)
+            banks = [(0, n) for n in range(4)]
+            return transpose_round(w1_sb[s], 1024, banks, w1_codes, w1_scales, 0, engines, late)
 
-        def views_round(s, gp, engines, late, fine):
+        def views_round(s, gp, tiles, engines, late, fine):
             wv_codes, wv_scales = wv_q[(s, gp)]
-            v_grouped = pair.tile([P, 2048], BF16, tag="v_grouped%d" % gp, align_bytes=64)
-            v_codes = pair.tile([P, 512], U32, tag="v_codes%d" % gp, align_bytes=64)
-            v_scales = pair.tile([P, 512], U8, tag="v_scales%d" % gp, align_bytes=64)
-            views_q[(s, gp)] = (v_codes, v_scales)
+            if (s, gp) not in views_q:
+                v_grouped = pair.tile([P, 2048], BF16, tag="v_grouped%d" % gp, align_bytes=64)
+                v_codes = pair.tile([P, 512], U32, tag="v_codes%d" % gp, align_bytes=64)
+                v_scales = pair.tile([P, 512], U8, tag="v_scales%d" % gp, align_bytes=64)
+                views_q[(s, gp)] = (v_codes, v_scales, v_grouped)
+            codes, scales, grouped = views_q[(s, gp)]
 
             def quantise(j0, j1):
                 nc.vector.quantize_mx(
-                    out=v_codes[:, 128 * j0 : 128 * j1].bitcast(FP8X4),
-                    scales=v_scales[:, 128 * j0 : 128 * j1],
-                    in_=v_grouped[:, 512 * j0 : 512 * j1],
+                    out=codes[:, 128 * j0 : 128 * j1].bitcast(FP8X4),
+                    scales=scales[:, 128 * j0 : 128 * j1],
+                    in_=grouped[:, 512 * j0 : 512 * j1],
                 )
 
-            for n in range(4):
-                half, tp = n // 2, n % 2
+            for n, j in enumerate(tiles):
                 bank = psum.tile([P, 512], F32, tag="bank")
-                for i in range(2):
-                    t = 2 * tp + i
+                for t in range(4):
                     for g in range(2):
-                        wc = slice(512 * g + 128 * t, 512 * g + 128 * (t + 1))
-                        hc = slice(512 * g + 256 * half, 512 * g + 256 * (half + 1))
+                        wc = slice(column(t, g), column(t, g) + 128)
+                        hc = slice(column(j, g), column(j, g) + 128)
                         nc.tensor.matmul_mx(
-                            out=bank[:, 256 * i : 256 * (i + 1)],
+                            out=bank[:, 128 * t : 128 * (t + 1)],
                             lhsT=wv_codes[:, wc].bitcast(FP8X4),
                             lhsT_scale=wv_scales[:, wc],
                             rhs=h_codes[:, hc].bitcast(FP8X4),
@@ -167,19 +177,17 @@ def tile_distributedb_pa_kernel(tc, x, h, Wv, W1, out):
                         )
                 copy_out(
                     engines[n],
-                    v_grouped[:, 1024 * half : 1024 * (half + 1)].rearrange("p (c t) -> p c t", t=4)[
-                        :, :, 2 * tp : 2 * tp + 2
-                    ],
-                    bank[:].rearrange("p (t c) -> p c t", t=2),
+                    grouped[:, 512 * j : 512 * (j + 1)].rearrange("p (c t) -> p c t", t=4),
+                    bank[:].rearrange("p (t c) -> p c t", t=4),
                 )
                 if n == 0:
                     flush(late)
-                if fine and n == 2:
-                    quantise(0, 2)
+                if fine and n > 0:
+                    quantise(j - 1, j)
             if fine:
-                quantise(2, 4)
+                quantise(tiles[-1], tiles[-1] + 1)
                 return None
-            return lambda: quantise(0, 4)
+            return lambda: quantise(tiles[0], tiles[-1] + 1)
 
         def out_round(s, late, fine):
             w1_codes, w1_scales = w1_q[s]
@@ -190,8 +198,8 @@ def tile_distributedb_pa_kernel(tc, x, h, Wv, W1, out):
                 if fine or j % 2 == 0:
                     bank = psum.tile([P, 512], F32, tag="bank")
                 c0 = 0 if fine else 256 * (j % 2)
-                operands = [(x_codes, x_scales, 512 * g + 128 * j) for g in range(2)]
-                operands.extend([views_q[(s, gp)] + (128 * j,) for gp in range(2)])
+                operands = [(x_codes, x_scales, column(j, g)) for g in range(2)]
+                operands.extend([views_q[(s, gp)][0:2] + (128 * j,) for gp in range(2)])
                 for n, (codes, scales, col) in enumerate(operands):
                     nc.tensor.matmul_mx(
                         out=bank[:, c0 : c0 + 256],
@@ -216,24 +224,30 @@ def tile_distributedb_pa_kernel(tc, x, h, Wv, W1, out):
             return None
 
         T_ENG = "VSSS"
-        V_ENG = "VVSS"
-        flush(transpose_round(h_sb, 512, four_tiles(0), h_codes, h_scales, "VSVS", None))
-        flush(wv_round(0, 0, "VSVS", None))
-        late = wv_round(0, 1, "VSVS", None)
-        late = views_round(0, 0, V_ENG, late, False)
-        late = wv_round(1, 0, T_ENG, late)
-        late = views_round(0, 1, V_ENG, late, False)
+        V_ENG = "VSVS"
+        ALL = [0, 1, 2, 3]
+        flush(rows_round(h_sb, h_codes, h_scales, [0], "VS", None))
+        flush(wv_round(0, 0, [0], "VS", None))
+        flush(wv_round(0, 0, [1], "VS", None))
+        flush(rows_round(h_sb, h_codes, h_scales, [1], "VS", None))
+        flush(wv_round(0, 1, [0], "VS", None))
+        late = views_round(0, 0, [0, 1], "VS", None, False)
+        flush(wv_round(0, 1, [1], "VS", late))
+        late = views_round(0, 0, [2, 3], "VS", None, False)
+        late = rows_round(x_sb, x_codes, x_scales, [0, 1], T_ENG, late)
         late = w1_round(0, T_ENG, late)
-        late = transpose_round(x_sb, 512, four_tiles(0), x_codes, x_scales, T_ENG, late)
+        late = views_round(0, 1, ALL, V_ENG, late, False)
         for s in range(1, NS):
-            late = views_round(s, 0, V_ENG, late, False)
-            late = wv_round(s, 1, T_ENG, late)
-            late = out_round(s - 1, late, False)
-            if s + 1 < NS:
-                late = wv_round(s + 1, 0, T_ENG, late)
-                late = views_round(s, 1, V_ENG, late, False)
+            if s == 2:
+                late = w1_round(1, T_ENG, late)
+            late = wv_round(s, 0, [0, 1], T_ENG, late)
+            late = wv_round(s, 1, [0, 1], T_ENG, late)
+            if s >= 2:
                 late = w1_round(s, T_ENG, late)
+            late = out_round(s - 1, late, False)
+            late = views_round(s, 0, ALL, V_ENG, late, False)
+            if s < NS - 1:
+                late = views_round(s, 1, ALL, V_ENG, late, False)
             else:
-                flush(w1_round(s, T_ENG, late))
-                views_round(s, 1, "SSVV", None, True)
+                views_round(s, 1, ALL, "SSSV", late, True)
         out_round(NS - 1, None, True)

from contextlib import ExitStack

import concourse.mybir as mybir
from concourse.masks import make_identity

F32 = mybir.dt.float32
BF16 = mybir.dt.bfloat16
U32 = mybir.dt.uint32
U8 = mybir.dt.uint8
FP8X4 = mybir.dt.float8_e4m3fn_x4
SILU = mybir.ActivationFunctionType.Silu

P = 128
NS = 4
R = 512
D = 1024
DV = 1024
SD = 256
FLOPS = 2 * NS * R * (D * DV + (D + DV) * SD)


def tile_distributedb_pa_kernel(tc, x, h, Wv, W1, out):
    nc = tc.nc
    with ExitStack() as ctx:
        const = ctx.enter_context(tc.tile_pool(name="const", bufs=1))
        inputs = ctx.enter_context(tc.tile_pool(name="inputs", bufs=1))
        stage = ctx.enter_context(tc.tile_pool(name="stage", bufs=3))
        keep = ctx.enter_context(tc.tile_pool(name="keep", bufs=1))
        pair = ctx.enter_context(tc.tile_pool(name="pair", bufs=2))
        psum = ctx.enter_context(tc.psum_pool(name="psum", bufs=8))
        ctx.enter_context(tc.manual_schedule())

        h_sb = inputs.tile([P, 4 * D], BF16, name="h_sb")
        x_sb = inputs.tile([P, 4 * D], BF16, name="x_sb")
        wv_sb = [inputs.tile([P, 8 * D], BF16, name="wv_sb%d" % s) for s in range(NS)]
        w1_sb = [inputs.tile([P, 2 * (D + DV)], BF16, name="w1_sb%d" % s) for s in range(NS)]

        def load_rows(dst, src, half):
            view = src.flatten_outer_dims().rearrange("(m j) d -> m (j d)", j=4)
            cols = slice(2 * D * half, 2 * D * (half + 1))
            nc.sync.dma_start(out=dst[:, cols], in_=view[:, cols])

        def load_wv(s, gp):
            for u in range(2):
                first = 512 * gp + 256 * u
                tile0 = 4 * gp + 2 * u
                nc.sync.dma_start(
                    out=wv_sb[s][:, tile0 * D : (tile0 + 2) * D],
                    in_=Wv[s, first : first + 256, :].rearrange("(m e) d -> m (e d)", e=2),
                )

        def load_w1(s):
            for half in range(2):
                cols = slice(D * half, D * (half + 1))
                nc.sync.dma_start(
                    out=w1_sb[s][:].rearrange("m (a k) -> m a k", a=2)[:, :, cols],
                    in_=W1[s].rearrange("(a m) k -> m a k", a=2)[:, :, cols],
                )

        load_rows(h_sb, h, 0)
        load_wv(0, 0)
        load_rows(h_sb, h, 1)
        load_wv(0, 1)
        load_rows(x_sb, x, 0)
        load_rows(x_sb, x, 1)
        load_w1(0)
        for s in range(1, NS):
            load_wv(s, 0)
            load_wv(s, 1)
            load_w1(s)

        ident = const.tile([P, P], F32, name="ident")
        make_identity(nc, ident[:])
        zero = const.tile([P, 1], F32, name="zero")
        nc.vector.memset(zero[:], 0.0)
        warm = const.tile([P, 1], F32, name="warm")
        nc.scalar.activation(out=warm[:], in_=zero[:], func=SILU)

        def copy_out(engine, dst, src):
            if engine == "V":
                nc.vector.tensor_copy(out=dst, in_=src)
            else:
                nc.scalar.copy(out=dst, in_=src)

        def flush(late):
            if late is not None:
                late()

        def transpose_round(src, tile_words, banks, codes, scales, col0, engines, late):
            words = src[:].bitcast(F32)
            n_banks = len(banks)
            grouped = stage.tile([P, 1024 * n_banks], BF16, tag="grouped", align_bytes=64)
            grouped_words = grouped[:].bitcast(F32)
            for n, (first_tile, k_pass) in enumerate(banks):
                bank = psum.tile([P, 512], F32, tag="bank")
                for u in range(2):
                    for i in range(2):
                        w0 = (first_tile + i) * tile_words + 256 * k_pass + 128 * u
                        c0 = 256 * u + 128 * i
                        nc.tensor.transpose(bank[:, c0 : c0 + 128], words[:, w0 : w0 + 128], ident[:])
                copy_out(
                    engines[n],
                    grouped_words[:, 512 * n : 512 * (n + 1)].rearrange("p (c u) -> p c u", u=2),
                    bank[:].rearrange("p (u c) -> p c u", u=2),
                )
                if n == 0:
                    flush(late)
            cols = slice(col0, col0 + 256 * n_banks)
            return lambda: nc.vector.quantize_mx(
                out=codes[:, cols].bitcast(FP8X4), scales=scales[:, cols], in_=grouped[:]
            )

        def tile_pairs(tile0, pairs):
            return [(tile0 + 2 * q, g) for q in pairs for g in range(2)]

        def column(tile, g):
            return 512 * (tile // 2) + 256 * g + 128 * (tile % 2)

        h_codes = keep.tile([P, 1024], U32, name="h_codes", align_bytes=64)
        h_scales = keep.tile([P, 1024], U8, name="h_scales", align_bytes=64)
        x_codes = keep.tile([P, 1024], U32, name="x_codes", align_bytes=64)
        x_scales = keep.tile([P, 1024], U8, name="x_scales", align_bytes=64)
        wv_q = {}
        w1_q = {}
        views_q = {}

        def rows_round(src, codes, scales, pairs, engines, late):
            return transpose_round(src, 512, tile_pairs(0, pairs), codes, scales, 512 * pairs[0], engines, late)

        def wv_round(s, gp, pairs, engines, late):
            if (s, gp) not in wv_q:
                wv_codes = pair.tile([P, 1024], U32, tag="wv_codes%d" % gp, align_bytes=64)
                wv_scales = pair.tile([P, 1024], U8, tag="wv_scales%d" % gp, align_bytes=64)
                wv_q[(s, gp)] = (wv_codes, wv_scales)
            codes, scales = wv_q[(s, gp)]
            return transpose_round(
                wv_sb[s], 512, tile_pairs(4 * gp, pairs), codes, scales, 512 * pairs[0], engines, late
            )

        def w1_round(s, engines, late):
            w1_codes = pair.tile([P, 1024], U32, tag="w1_codes", align_bytes=64)
            w1_scales = pair.tile([P, 1024], U8, tag="w1_scales", align_bytes=64)
            w1_q[s] = (w1_codes, w1_scales)
            banks = [(0, n) for n in range(4)]
            return transpose_round(w1_sb[s], 1024, banks, w1_codes, w1_scales, 0, engines, late)

        def views_round(s, gp, tiles, engines, late, fine):
            wv_codes, wv_scales = wv_q[(s, gp)]
            if (s, gp) not in views_q:
                v_grouped = pair.tile([P, 2048], BF16, tag="v_grouped%d" % gp, align_bytes=64)
                v_codes = pair.tile([P, 512], U32, tag="v_codes%d" % gp, align_bytes=64)
                v_scales = pair.tile([P, 512], U8, tag="v_scales%d" % gp, align_bytes=64)
                views_q[(s, gp)] = (v_codes, v_scales, v_grouped)
            codes, scales, grouped = views_q[(s, gp)]

            def quantise(j0, j1):
                nc.vector.quantize_mx(
                    out=codes[:, 128 * j0 : 128 * j1].bitcast(FP8X4),
                    scales=scales[:, 128 * j0 : 128 * j1],
                    in_=grouped[:, 512 * j0 : 512 * j1],
                )

            for n, j in enumerate(tiles):
                bank = psum.tile([P, 512], F32, tag="bank")
                for t in range(4):
                    for g in range(2):
                        wc = slice(column(t, g), column(t, g) + 128)
                        hc = slice(column(j, g), column(j, g) + 128)
                        nc.tensor.matmul_mx(
                            out=bank[:, 128 * t : 128 * (t + 1)],
                            lhsT=wv_codes[:, wc].bitcast(FP8X4),
                            lhsT_scale=wv_scales[:, wc],
                            rhs=h_codes[:, hc].bitcast(FP8X4),
                            rhs_scale=h_scales[:, hc],
                            start=(g == 0),
                            stop=(g == 1),
                        )
                copy_out(
                    engines[n],
                    grouped[:, 512 * j : 512 * (j + 1)].rearrange("p (c t) -> p c t", t=4),
                    bank[:].rearrange("p (t c) -> p c t", t=4),
                )
                if n == 0:
                    flush(late)
                if fine and n > 0:
                    quantise(j - 1, j)
            if fine:
                quantise(tiles[-1], tiles[-1] + 1)
                return None
            return lambda: quantise(tiles[0], tiles[-1] + 1)

        def out_round(s, late, fine):
            w1_codes, w1_scales = w1_q[s]
            o_sb = pair.tile([P, 4 * SD], F32, tag="o_sb")
            o_view = out[s].rearrange("b q f -> (b q) f").rearrange("(m j) f -> m (j f)", j=4)
            bank = None
            for j in range(4):
                if fine or j % 2 == 0:
                    bank = psum.tile([P, 512], F32, tag="bank")
                c0 = 0 if fine else 256 * (j % 2)
                operands = [(x_codes, x_scales, column(j, g)) for g in range(2)]
                operands.extend([views_q[(s, gp)][0:2] + (128 * j,) for gp in range(2)])
                for n, (codes, scales, col) in enumerate(operands):
                    nc.tensor.matmul_mx(
                        out=bank[:, c0 : c0 + 256],
                        lhsT=codes[:, col : col + 128].bitcast(FP8X4),
                        lhsT_scale=scales[:, col : col + 128],
                        rhs=w1_codes[:, 256 * n : 256 * (n + 1)].bitcast(FP8X4),
                        rhs_scale=w1_scales[:, 256 * n : 256 * (n + 1)],
                        start=(n == 0),
                        stop=(n == 3),
                    )
                if fine:
                    cols = slice(256 * j, 256 * (j + 1))
                    nc.scalar.activation(out=o_sb[:, cols], in_=bank[:, 0:256], func=SILU)
                    nc.sync.dma_start(out=o_view[:, cols], in_=o_sb[:, cols])
                elif j % 2 == 1:
                    cols = slice(256 * (j - 1), 256 * (j + 1))
                    nc.scalar.activation(out=o_sb[:, cols], in_=bank[:], func=SILU)
                if j == 1:
                    flush(late)
            if not fine:
                nc.sync.dma_start(out=o_view, in_=o_sb[:])
            return None

        T_ENG = "VSSS"
        V_ENG = "VSVS"
        ALL = [0, 1, 2, 3]
        flush(rows_round(h_sb, h_codes, h_scales, [0], "VS", None))
        flush(wv_round(0, 0, [0], "VS", None))
        flush(wv_round(0, 0, [1], "VS", None))
        flush(rows_round(h_sb, h_codes, h_scales, [1], "VS", None))
        flush(wv_round(0, 1, [0], "VS", None))
        late = views_round(0, 0, [0, 1], "VS", None, False)
        flush(wv_round(0, 1, [1], "VS", late))
        late = views_round(0, 0, [2, 3], "VS", None, False)
        late = rows_round(x_sb, x_codes, x_scales, [0, 1], T_ENG, late)
        late = w1_round(0, T_ENG, late)
        late = views_round(0, 1, ALL, V_ENG, late, False)
        for s in range(1, NS):
            if s == 2:
                late = w1_round(1, T_ENG, late)
            late = wv_round(s, 0, [0, 1], T_ENG, late)
            late = wv_round(s, 1, [0, 1], T_ENG, late)
            if s >= 2:
                late = w1_round(s, T_ENG, late)
            late = out_round(s - 1, late, False)
            late = views_round(s, 0, ALL, V_ENG, late, False)
            if s < NS - 1:
                late = views_round(s, 1, ALL, V_ENG, late, False)
            else:
                views_round(s, 1, ALL, "SSSV", late, True)
        out_round(NS - 1, None, True)
